import numpy as np
import ml_dtypes


def mxq(x, axis, fmt="e4m3"):
    dtype, down = {"e4m3": (ml_dtypes.float8_e4m3fn, 7), "e5m2": (ml_dtypes.float8_e5m2, 14)}[fmt]
    v = np.moveaxis(np.asarray(x, np.float32).astype(ml_dtypes.bfloat16).astype(np.float64), axis, -1)
    blocks = v.reshape(v.shape[:-1] + (-1, 32))
    amax = np.abs(blocks).max(-1, keepdims=True)
    byte = np.maximum(np.where(amax > 0, np.frexp(amax)[1] - 1 + 127, 0) - down, 1)
    scale = np.exp2(byte - 127.0)
    codes = (blocks / scale).astype(np.float32).astype(dtype).astype(np.float64)
    return np.moveaxis((codes * scale).reshape(v.shape), -1, axis)


WIDE = False


def mx_kscale(k):
    if not WIDE:
        return np.ones(k)
    levels = np.array([10, -10, 5, -5, 0])
    if k % 512:
        return np.exp2(np.random.permutation(np.resize(levels, k // 32))).repeat(32)
    a = np.empty((k // 512, 16))
    for p in range(k // 512):
        a[p, :8] = np.random.permutation(np.resize(levels, 8))
        for g in range(8):
            far = levels[np.abs(levels - a[p, g]) >= 10]
            a[p, g + 8] = far[np.random.randint(len(far))]
    return np.exp2(a.ravel()).repeat(32)


BF16 = ml_dtypes.bfloat16


def bf(x):
    return np.asarray(x, np.float32).astype(BF16)


def f64(x):
    return np.asarray(x).astype(np.float64)


B, S, D, K = 512, 8, 1024, 512


def setup_inputs():
    t = np.exp2(np.round(np.log2(mx_kscale(D)) / 2))
    q = np.random.standard_normal((B, S, D))
    a = 0.3 * np.random.standard_normal((B, S, 1))
    p = np.random.standard_normal((B, S, D)) + a * q[:, -1:, :]
    W = np.random.uniform(0.0, 1.0, (K, D)) * np.sqrt(12.0 / D)
    return {"p": bf(p / t), "q": bf(q / t), "W": bf(W * t)}


def reference(p, q, W):
    p, q, W = f64(p), f64(q), f64(W)
    W2 = mxq(W * W, 1, "e4m3")
    q_last = q[:, -1, :]
    dot = (mxq(p * q_last[:, None, :], 2, "e4m3") @ W2.T).transpose(0, 2, 1)
    norm_p = np.sqrt((mxq(p * p, 2, "e4m3") @ W2.T).transpose(0, 2, 1))
    norm_q = np.sqrt(mxq(q_last * q_last, 1, "e4m3") @ W2.T)
    dist = -dot / (norm_p * norm_q[:, :, None] * D)
    return dist.reshape(B, S, -1)

@@ -1,0 +1,377 @@
+from contextlib import ExitStack
+
+import concourse.mybir as mybir
+from concourse.masks import make_identity
+
+F32 = mybir.dt.float32
+BF16 = mybir.dt.bfloat16
+U32 = mybir.dt.uint32
+U8 = mybir.dt.uint8
+FP8X4 = mybir.dt.float8_e4m3fn_x4
+FN = mybir.ActivationFunctionType
+ALU = mybir.AluOpType
+
+P = 128
+B, S, D, K = 512, 8, 1024, 512
+NBT = B // P
+NKT = K // P
+SH = 4
+HALVES = S // SH
+ROUNDS = NBT * HALVES
+PASSES = D // 512
+WORDS = D // 4
+
+FLOPS = 2 * (2 * B * S + B) * K * D
+BYTES = 2 * (B * S * D + B * D + K * D) + 4 * B * S * K
+
+PINNED = True
+HALF_K = K // 2
+VECTOR_K = 64
+
+
+def tile_mpl_t_kernel(tc, p, q, W, out):
+    nc = tc.nc
+    out_flat = out.rearrange("b s k -> b (s k)")
+    with ExitStack() as ctx:
+        if PINNED:
+            ctx.enter_context(tc.manual_schedule())
+        const = ctx.enter_context(tc.tile_pool(name="const", bufs=1))
+        loads = ctx.enter_context(tc.tile_pool(name="loads", bufs=6))
+        prods = ctx.enter_context(tc.tile_pool(name="prods", bufs=2))
+        epi = ctx.enter_context(tc.tile_pool(name="epi", bufs=2))
+        outs = ctx.enter_context(tc.tile_pool(name="outs", bufs=2))
+        psx = ctx.enter_context(tc.psum_pool(name="psx", bufs=4))
+        psn = ctx.enter_context(tc.psum_pool(name="psn", bufs=2))
+        psd = ctx.enter_context(tc.psum_pool(name="psd", bufs=2))
+
+        one = const.tile([P, 1], F32, name="one")
+        warm = const.tile([P, 1], F32, name="warm")
+        nc.vector.memset(one[:], 1.0)
+        nc.scalar.activation(out=warm[:], in_=one[:], func=FN.Abs_reciprocal_sqrt)
+
+        ident = const.tile([P, P], F32, name="ident")
+        make_identity(nc, ident[:])
+
+        w_ld = const.tile([P, NKT * D], BF16, name="w_ld")
+        q_ld = const.tile([P, NBT * D], BF16, name="q_ld")
+        p_ld = []
+
+        def load_q(bt):
+            nc.sync.dma_start(out=q_ld[:, bt * D:(bt + 1) * D], in_=q[bt * P:(bt + 1) * P, S - 1, :])
+
+        def load_p(r, pieces):
+            bt, sh = divmod(r, HALVES)
+            ld = loads.tile([P, SH * D], BF16, name="ld")
+            n = SH // pieces
+            for i in range(pieces):
+                nc.sync.dma_start(
+                    out=ld[:, i * n * D:(i + 1) * n * D],
+                    in_=p[bt * P:(bt + 1) * P, sh * SH + i * n:sh * SH + (i + 1) * n, :].rearrange(
+                        "b s d -> b (s d)"
+                    ),
+                )
+            p_ld.append(ld)
+
+        for kt in range(NKT):
+            nc.sync.dma_start(out=w_ld[:, kt * D:(kt + 1) * D], in_=W[kt * P:(kt + 1) * P, :])
+        load_q(0)
+        load_p(0, SH)
+        load_p(1, 1)
+        for bt in range(1, NBT):
+            load_q(bt)
+        for r in range(2, ROUNDS):
+            load_p(r, 1)
+
+        w_sq = const.tile([P, NKT * D], BF16, name="w_sq", align_bytes=64)
+        w_codes = const.tile([P, NKT * WORDS], U32, name="w_codes", align_bytes=64)
+        w_scales = const.tile([P, NKT * WORDS], U8, name="w_scales", align_bytes=64)
+        w_raw = const.tile([P, 2 * D], BF16, name="w_raw")
+        q_raw = const.tile([P, NBT * D], BF16, name="q_raw")
+        q_sq = const.tile([P, NBT * D], BF16, name="q_sq", align_bytes=64)
+        q_codes = const.tile([P, NBT * WORDS], U32, name="q_codes", align_bytes=64)
+        q_scales = const.tile([P, NBT * WORDS], U8, name="q_scales", align_bytes=64)
+        factor = const.tile([P, NBT * K], F32, name="factor")
+
+        banks = {}
+        tiles = {}
+
+        def unit(ap, i):
+            return ap[:, i * D:(i + 1) * D]
+
+        def transposes(key, src):
+            xt = psx.tile([P, 512], F32, name="xt")
+            words = src.bitcast(F32)
+            for g in range(PASSES):
+                for u in range(2):
+                    nc.tensor.transpose(
+                        out=xt[:, u * 256 + g * P:u * 256 + (g + 1) * P],
+                        in_=words[:, g * 256 + u:(g + 1) * 256:2],
+                        identity=ident[:],
+                    )
+            banks[key] = xt
+
+        def t_p(r, sl):
+            transposes(("p", r, sl), unit(p_ld[r], sl))
+
+        def bank_values(key):
+            return banks[key][:].bitcast(BF16).rearrange("p (u c e) -> p c u e", u=2, e=2)
+
+        def grouped(ap):
+            return ap.rearrange("p (c u e) -> p c u e", u=2, e=2)
+
+        def copy_words(key, dst, on_scalar):
+            copy = nc.scalar.copy if on_scalar else nc.vector.tensor_copy
+            copy(
+                out=dst.bitcast(F32).rearrange("p (c u) -> p c u", u=2),
+                in_=banks[key][:].rearrange("p (u c) -> p c u", u=2),
+            )
+
+        def square_bank(key, dst):
+            nc.scalar.activation(out=grouped(dst), in_=bank_values(key), func=FN.Square)
+
+        def quantise(src, codes, scales, first, count):
+            nc.vector.quantize_mx(
+                out=codes[:, first * WORDS:(first + count) * WORDS].bitcast(FP8X4),
+                scales=scales[:, first * WORDS:(first + count) * WORDS],
+                in_=src[:, first * D:(first + count) * D],
+            )
+
+        def mx_group(dst, a_codes, a_scales, a_unit, kt):
+            for g in range(PASSES):
+                a0 = a_unit * WORDS + g * P
+                w0 = kt * WORDS + g * P
+                nc.tensor.matmul_mx(
+                    out=dst,
+                    lhsT=a_codes[:, a0:a0 + P].bitcast(FP8X4),
+                    lhsT_scale=a_scales[:, a0:a0 + P],
+                    rhs=w_codes[:, w0:w0 + P].bitcast(FP8X4),
+                    rhs_scale=w_scales[:, w0:w0 + P],
+                    start=(g == 0),
+                    stop=(g == PASSES - 1),
+                )
+
+        def q_copy(bt):
+            copy_words(("q", bt), unit(q_raw, bt), bt > 0)
+
+        def q_square(bt):
+            nc.vector.tensor_tensor(out=unit(q_sq, bt), in0=unit(q_raw, bt), in1=unit(q_raw, bt), op=ALU.mult)
+
+        def q_quantise(bt):
+            quantise(q_sq, q_codes, q_scales, bt, 1)
+
+        def q_norms(bt):
+            nq = psn.tile([P, K], F32, name="npb")
+            for kt in range(NKT):
+                mx_group(nq[:, kt * P:(kt + 1) * P], q_codes, q_scales, bt, kt)
+            banks[("nq", bt)] = nq
+
+        def q_factor(bt):
+            f = factor[:, bt * K:(bt + 1) * K]
+            nc.scalar.activation(out=f, in_=banks[("nq", bt)][:], func=FN.Abs_reciprocal_sqrt)
+
+        def round_tile(r, name, shape, dtype):
+            if (name, r) not in tiles:
+                tiles[(name, r)] = prods.tile(shape, dtype, name=name, align_bytes=64)
+            return tiles[(name, r)]
+
+        def prod_of(r):
+            return round_tile(r, "prod", [P, 2 * SH * D], BF16)
+
+        def pp_unit(sl):
+            return (sl // 2) * 4 + sl % 2
+
+        def pq_unit(sl):
+            return (sl // 2) * 4 + 2 + sl % 2
+
+        def sq(r, sl):
+            square_bank(("p", r, sl), unit(prod_of(r), pp_unit(sl)))
+
+        def pq(r, sl):
+            nc.vector.tensor_tensor(
+                out=grouped(unit(prod_of(r), pq_unit(sl))),
+                in0=bank_values(("p", r, sl)),
+                in1=grouped(unit(q_raw, r // HALVES)),
+                op=ALU.mult,
+            )
+
+        def quant(r, half):
+            quantise(
+                prod_of(r),
+                round_tile(r, "codes", [P, 2 * SH * WORDS], U32),
+                round_tile(r, "scales", [P, 2 * SH * WORDS], U8),
+                4 * half,
+                4,
+            )
+
+        def mx(r, kt):
+            codes = tiles[("codes", r)]
+            scales = tiles[("scales", r)]
+            dtb = psd.tile([P, SH * P], F32, name="dtb")
+            for sl in range(SH):
+                mx_group(dtb[:, sl * P:(sl + 1) * P], codes, scales, pq_unit(sl), kt)
+            npb = psn.tile([P, SH * P], F32, name="npb")
+            for sl in range(SH):
+                mx_group(npb[:, sl * P:(sl + 1) * P], codes, scales, pp_unit(sl), kt)
+            banks[("dot", r, kt)] = dtb
+            banks[("np", r, kt)] = npb
+
+        def epi_tile(r, name):
+            if (name, r) not in tiles:
+                tiles[(name, r)] = epi.tile([P, K * SH], F32, name=name)
+            return tiles[(name, r)]
+
+        def ks(ap, s):
+            return ap.rearrange("p (k s) -> p k s", s=s)
+
+        def chunk(ap, kt):
+            return ks(ap[:, kt * P * SH:(kt + 1) * P * SH], SH)
+
+        def rs(r, kt):
+            nc.scalar.activation(
+                out=chunk(epi_tile(r, "rn"), kt),
+                in_=banks[("np", r, kt)][:].rearrange("p (s k) -> p k s", s=SH),
+                func=FN.Abs_reciprocal_sqrt,
+            )
+
+        def dc(r, kt):
+            bt = r // HALVES
+            nc.vector.scalar_tensor_tensor(
+                out=chunk(epi_tile(r, "dc"), kt),
+                in0=banks[("dot", r, kt)][:].rearrange("p (s k) -> p k s", s=SH),
+                scalar=-1.0 / D,
+                in1=factor[:, bt * K + kt * P:bt * K + (kt + 1) * P].unsqueeze(2).to_broadcast([P, P, SH]),
+                op0=ALU.mult,
+                op1=ALU.mult,
+            )
+
+        def fin_part(eng, r, k0, k1):
+            bt, sh = divmod(r, HALVES)
+            if ("o", bt) not in tiles:
+                tiles[("o", bt)] = outs.tile([P, K * S], F32, name="o_sb")
+            eng.tensor_tensor(
+                out=ks(tiles[("o", bt)][:, k0 * S:k1 * S], S)[:, :, sh * SH:(sh + 1) * SH],
+                in0=ks(tiles[("dc", r)][:, k0 * SH:k1 * SH], SH),
+                in1=ks(tiles[("rn", r)][:, k0 * SH:k1 * SH], SH),
+                op=ALU.mult,
+            )
+
+        def fin(r, h):
+            bt, sh = divmod(r, HALVES)
+            if bt == NBT - 1:
+                return
+            fin_part(nc.vector, r, h * HALF_K, h * HALF_K + VECTOR_K)
+            fin_part(nc.gpsimd, r, h * HALF_K + VECTOR_K, (h + 1) * HALF_K)
+            if sh == HALVES - 1:
+                cols = slice(h * HALF_K * S, (h + 1) * HALF_K * S)
+                nc.sync.dma_start(out=out_flat[bt * P:(bt + 1) * P, cols], in_=tiles[("o", bt)][:, cols])
+
+        def fin_last(r, kt):
+            fin_part(nc.vector, r, kt * P, (kt + 1) * P)
+            if r == ROUNDS - 1:
+                cols = slice(kt * P * S, (kt + 1) * P * S)
+                nc.sync.dma_start(
+                    out=out_flat[(NBT - 1) * P:NBT * P, cols], in_=tiles[("o", NBT - 1)][:, cols]
+                )
+
+        for kt in range(NKT):
+            transposes(("w", kt), unit(w_ld, kt))
+        for kt in range(NKT):
+            if kt % 2 == 0:
+                copy_words(("w", kt), unit(w_raw, kt // 2), False)
+                nc.vector.tensor_tensor(
+                    out=unit(w_sq, kt), in0=unit(w_raw, kt // 2), in1=unit(w_raw, kt // 2), op=ALU.mult
+                )
+            else:
+                square_bank(("w", kt), unit(w_sq, kt))
+        transposes(("q", 0), unit(q_ld, 0))
+        t_p(0, 0)
+        t_p(0, 1)
+        t_p(0, 2)
+        q_copy(0)
+        q_square(0)
+        quantise(w_sq, w_codes, w_scales, 0, 2)
+        quantise(w_sq, w_codes, w_scales, 2, 2)
+        q_quantise(0)
+        t_p(0, 3)
+        sq(0, 0)
+        sq(0, 1)
+        pq(0, 0)
+        pq(0, 1)
+        t_p(1, 0)
+        t_p(1, 1)
+        q_norms(0)
+        sq(0, 2)
+        quant(0, 0)
+        sq(0, 3)
+        pq(0, 2)
+        pq(0, 3)
+        t_p(1, 2)
+        t_p(1, 3)
+
+        def period(r):
+            nxt = r + 1 < ROUNDS
+            bt = r // HALVES
+            early_q = r % HALVES == 0 and bt + 1 < NBT
+            late_q = r % HALVES == 1 and bt + 1 < NBT
+            if nxt:
+                sq(r + 1, 0)
+                sq(r + 1, 1)
+            if r == 0:
+                q_factor(0)
+            if nxt:
+                sq(r + 1, 2)
+            quant(r, 1)
+            if late_q:
+                q_square(bt + 1)
+            if r > 0:
+                fin(r - 1, 1)
+            if nxt:
+                pq(r + 1, 0)
+                pq(r + 1, 1)
+            else:
+                fin_last(r - 1, 0)
+            mx(r, 0)
+            mx(r, 1)
+            dc(r, 0)
+            if not nxt:
+                fin_last(r - 1, 1)
+            dc(r, 1)
+            rs(r, 0)
+            if nxt:
+                sq(r + 1, 3)
+            rs(r, 1)
+            if early_q:
+                transposes(("q", bt + 1), unit(q_ld, bt + 1))
+                q_copy(bt + 1)
+            if nxt:
+                quant(r + 1, 0)
+            if late_q:
+                q_quantise(bt + 1)
+            fin(r, 0)
+            if nxt:
+                pq(r + 1, 2)
+                pq(r + 1, 3)
+            else:
+                fin_last(r - 1, 2)
+                fin_last(r, 0)
+            mx(r, 2)
+            mx(r, 3)
+            dc(r, 2)
+            if not nxt:
+                fin_last(r - 1, 3)
+                fin_last(r, 1)
+            dc(r, 3)
+            rs(r, 2)
+            rs(r, 3)
+            if not nxt:
+                fin_last(r, 2)
+                fin_last(r, 3)
+            if late_q:
+                q_norms(bt + 1)
+                q_factor(bt + 1)
+            if r + 2 < ROUNDS:
+                for sl in range(SH):
+                    t_p(r + 2, sl)
+
+        for r in range(ROUNDS):
+            period(r)

@@ -25,7 +25,9 @@ FLOPS = 2 * (2 * B * S + B) * K * D
 BYTES = 2 * (B * S * D + B * D + K * D) + 4 * B * S * K
 
 PINNED = True
-HALF_K = K // 2
+KH = K // 2
+NKH = K // KH
+SB = SH // 2
 VECTOR_K = 64
 
 
@@ -110,6 +112,18 @@ def tile_mpl_t_kernel(tc, p, q, W, out):
                     )
             banks[key] = xt
 
+        def t_w(kh, g):
+            xt = psx.tile([P, 512], F32, name="xt")
+            for i in range(2):
+                words = unit(w_ld, 2 * kh + i).bitcast(F32)
+                for u in range(2):
+                    nc.tensor.transpose(
+                        out=xt[:, u * 256 + i * P:u * 256 + (i + 1) * P],
+                        in_=words[:, g * 256 + u:(g + 1) * 256:2],
+                        identity=ident[:],
+                    )
+            banks[("w", 2 * kh + g)] = xt
+
         def t_p(r, sl):
             transposes(("p", r, sl), unit(p_ld[r], sl))
 
@@ -136,16 +150,16 @@ def tile_mpl_t_kernel(tc, p, q, W, out):
                 in_=src[:, first * D:(first + count) * D],
             )
 
-        def mx_group(dst, a_codes, a_scales, a_unit, kt):
+        def mx_group(dst, a_codes, a_scales, a_unit, kh):
             for g in range(PASSES):
                 a0 = a_unit * WORDS + g * P
-                w0 = kt * WORDS + g * P
+                w0 = (kh * PASSES + g) * KH
                 nc.tensor.matmul_mx(
                     out=dst,
                     lhsT=a_codes[:, a0:a0 + P].bitcast(FP8X4),
                     lhsT_scale=a_scales[:, a0:a0 + P],
-                    rhs=w_codes[:, w0:w0 + P].bitcast(FP8X4),
-                    rhs_scale=w_scales[:, w0:w0 + P],
+                    rhs=w_codes[:, w0:w0 + KH].bitcast(FP8X4),
+                    rhs_scale=w_scales[:, w0:w0 + KH],
                     start=(g == 0),
                     stop=(g == PASSES - 1),
                 )
@@ -161,8 +175,8 @@ def tile_mpl_t_kernel(tc, p, q, W, out):
 
         def q_norms(bt):
             nq = psn.tile([P, K], F32, name="npb")
-            for kt in range(NKT):
-                mx_group(nq[:, kt * P:(kt + 1) * P], q_codes, q_scales, bt, kt)
+            for kh in range(NKH):
+                mx_group(nq[:, kh * KH:(kh + 1) * KH], q_codes, q_scales, bt, kh)
             banks[("nq", bt)] = nq
 
         def q_factor(bt):
@@ -203,17 +217,18 @@ def tile_mpl_t_kernel(tc, p, q, W, out):
                 4,
             )
 
-        def mx(r, kt):
+        def mx(r, x):
             codes = tiles[("codes", r)]
             scales = tiles[("scales", r)]
-            dtb = psd.tile([P, SH * P], F32, name="dtb")
-            for sl in range(SH):
-                mx_group(dtb[:, sl * P:(sl + 1) * P], codes, scales, pq_unit(sl), kt)
-            npb = psn.tile([P, SH * P], F32, name="npb")
-            for sl in range(SH):
-                mx_group(npb[:, sl * P:(sl + 1) * P], codes, scales, pp_unit(sl), kt)
-            banks[("dot", r, kt)] = dtb
-            banks[("np", r, kt)] = npb
+            kh, pair = divmod(x, 2)
+            dtb = psd.tile([P, SB * KH], F32, name="dtb")
+            for i in range(SB):
+                mx_group(dtb[:, i * KH:(i + 1) * KH], codes, scales, pq_unit(pair * SB + i), kh)
+            npb = psn.tile([P, SB * KH], F32, name="npb")
+            for i in range(SB):
+                mx_group(npb[:, i * KH:(i + 1) * KH], codes, scales, pp_unit(pair * SB + i), kh)
+            banks[("dot", r, x)] = dtb
+            banks[("np", r, x)] = npb
 
         def epi_tile(r, name):
             if (name, r) not in tiles:
@@ -223,23 +238,23 @@ def tile_mpl_t_kernel(tc, p, q, W, out):
         def ks(ap, s):
             return ap.rearrange("p (k s) -> p k s", s=s)
 
-        def chunk(ap, kt):
-            return ks(ap[:, kt * P * SH:(kt + 1) * P * SH], SH)
+        def part(ap, x):
+            return ks(ap[:, x * KH * SB:(x + 1) * KH * SB], SB)
 
-        def rs(r, kt):
+        def rs(r, x):
             nc.scalar.activation(
-                out=chunk(epi_tile(r, "rn"), kt),
-                in_=banks[("np", r, kt)][:].rearrange("p (s k) -> p k s", s=SH),
+                out=part(epi_tile(r, "rn"), x),
+                in_=banks[("np", r, x)][:].rearrange("p (s k) -> p k s", s=SB),
                 func=FN.Abs_reciprocal_sqrt,
             )
 
-        def dc(r, kt):
-            bt = r // HALVES
+        def dc(r, x):
+            f0 = r // HALVES * K + x // 2 * KH
             nc.vector.scalar_tensor_tensor(
-                out=chunk(epi_tile(r, "dc"), kt),
-                in0=banks[("dot", r, kt)][:].rearrange("p (s k) -> p k s", s=SH),
+                out=part(epi_tile(r, "dc"), x),
+                in0=banks[("dot", r, x)][:].rearrange("p (s k) -> p k s", s=SB),
                 scalar=-1.0 / D,
-                in1=factor[:, bt * K + kt * P:bt * K + (kt + 1) * P].unsqueeze(2).to_broadcast([P, P, SH]),
+                in1=factor[:, f0:f0 + KH].unsqueeze(2).to_broadcast([P, KH, SB]),
                 op0=ALU.mult,
                 op1=ALU.mult,
             )
@@ -248,10 +263,17 @@ def tile_mpl_t_kernel(tc, p, q, W, out):
             bt, sh = divmod(r, HALVES)
             if ("o", bt) not in tiles:
                 tiles[("o", bt)] = outs.tile([P, K * S], F32, name="o_sb")
+            kh = k0 // KH
+
+            def both_pairs(name):
+                half = tiles[(name, r)][:, kh * KH * SH:(kh + 1) * KH * SH]
+                return half.rearrange("p (a k s) -> p k a s", a=2, s=SB)[:, k0 - kh * KH:k1 - kh * KH]
+
+            o = ks(tiles[("o", bt)][:, k0 * S:k1 * S], S)[:, :, sh * SH:(sh + 1) * SH]
             eng.tensor_tensor(
-                out=ks(tiles[("o", bt)][:, k0 * S:k1 * S], S)[:, :, sh * SH:(sh + 1) * SH],
-                in0=ks(tiles[("dc", r)][:, k0 * SH:k1 * SH], SH),
-                in1=ks(tiles[("rn", r)][:, k0 * SH:k1 * SH], SH),
+                out=o.rearrange("p k (a s) -> p k a s", a=2),
+                in0=both_pairs("dc"),
+                in1=both_pairs("rn"),
                 op=ALU.mult,
             )
 
@@ -259,10 +281,10 @@ def tile_mpl_t_kernel(tc, p, q, W, out):
             bt, sh = divmod(r, HALVES)
             if bt == NBT - 1:
                 return
-            fin_part(nc.vector, r, h * HALF_K, h * HALF_K + VECTOR_K)
-            fin_part(nc.gpsimd, r, h * HALF_K + VECTOR_K, (h + 1) * HALF_K)
+            fin_part(nc.vector, r, h * KH, h * KH + VECTOR_K)
+            fin_part(nc.gpsimd, r, h * KH + VECTOR_K, (h + 1) * KH)
             if sh == HALVES - 1:
-                cols = slice(h * HALF_K * S, (h + 1) * HALF_K * S)
+                cols = slice(h * KH * S, (h + 1) * KH * S)
                 nc.sync.dma_start(out=out_flat[bt * P:(bt + 1) * P, cols], in_=tiles[("o", bt)][:, cols])
 
         def fin_last(r, kt):
@@ -274,7 +296,7 @@ def tile_mpl_t_kernel(tc, p, q, W, out):
                 )
 
         for kt in range(NKT):
-            transposes(("w", kt), unit(w_ld, kt))
+            t_w(kt // 2, kt % 2)
         for kt in range(NKT):
             if kt % 2 == 0:
                 copy_words(("w", kt), unit(w_raw, kt // 2), False)

@@ -28,7 +28,6 @@ PINNED = True
 KH = K // 2
 NKH = K // KH
 SB = SH // 2
-VECTOR_K = 64
 
 
 def tile_mpl_t_kernel(tc, p, q, W, out):
@@ -279,15 +278,20 @@ def tile_mpl_t_kernel(tc, p, q, W, out):
 
         def fin(r, h):
             bt, sh = divmod(r, HALVES)
-            if bt == NBT - 1:
+            if r == ROUNDS - 1:
                 return
-            fin_part(nc.vector, r, h * KH, h * KH + VECTOR_K)
-            fin_part(nc.gpsimd, r, h * KH + VECTOR_K, (h + 1) * KH)
+            fin_part(nc.gpsimd, r, h * KH, (h + 1) * KH)
             if sh == HALVES - 1:
                 cols = slice(h * KH * S, (h + 1) * KH * S)
                 nc.sync.dma_start(out=out_flat[bt * P:(bt + 1) * P, cols], in_=tiles[("o", bt)][:, cols])
 
+        def after_gpsimd(r, k):
+            c0 = k * S + r % HALVES * SH
+            nc.vector.tensor_copy(out=warm[:], in_=tiles[("o", r // HALVES)][:, c0:c0 + 1])
+
         def fin_last(r, kt):
+            if kt % 2 == 0:
+                after_gpsimd(r - 1, kt * P)
             fin_part(nc.vector, r, kt * P, (kt + 1) * P)
             if r == ROUNDS - 1:
                 cols = slice(kt * P * S, (kt + 1) * P * S)
@@ -298,7 +302,7 @@ def tile_mpl_t_kernel(tc, p, q, W, out):
         for kt in range(NKT):
             t_w(kt // 2, kt % 2)
         for kt in range(NKT):
-            if kt % 2 == 0:
+            if kt == 2:
                 copy_words(("w", kt), unit(w_raw, kt // 2), False)
                 nc.vector.tensor_tensor(
                     out=unit(w_sq, kt), in0=unit(w_raw, kt // 2), in1=unit(w_raw, kt // 2), op=ALU.mult
@@ -350,13 +354,9 @@ def tile_mpl_t_kernel(tc, p, q, W, out):
             if nxt:
                 pq(r + 1, 0)
                 pq(r + 1, 1)
-            else:
-                fin_last(r - 1, 0)
             mx(r, 0)
             mx(r, 1)
             dc(r, 0)
-            if not nxt:
-                fin_last(r - 1, 1)
             dc(r, 1)
             rs(r, 0)
             if nxt:
@@ -374,13 +374,11 @@ def tile_mpl_t_kernel(tc, p, q, W, out):
                 pq(r + 1, 2)
                 pq(r + 1, 3)
             else:
-                fin_last(r - 1, 2)
                 fin_last(r, 0)
             mx(r, 2)
             mx(r, 3)
             dc(r, 2)
             if not nxt:
-                fin_last(r - 1, 3)
                 fin_last(r, 1)
             dc(r, 3)
             rs(r, 2)

@@ -24,7 +24,9 @@ WORDS = D // 4
 FLOPS = 2 * (2 * B * S + B) * K * D
 BYTES = 2 * (B * S * D + B * D + K * D) + 4 * B * S * K
 
+LAST_K = 64
 PINNED = True
+VECTOR_K = 32
 KH = K // 2
 NKH = K // KH
 SB = SH // 2
@@ -240,10 +242,10 @@ def tile_mpl_t_kernel(tc, p, q, W, out):
         def part(ap, x):
             return ks(ap[:, x * KH * SB:(x + 1) * KH * SB], SB)
 
-        def rs(r, x):
+        def rs(r, x, k0=0, k1=KH):
             nc.scalar.activation(
-                out=part(epi_tile(r, "rn"), x),
-                in_=banks[("np", r, x)][:].rearrange("p (s k) -> p k s", s=SB),
+                out=part(epi_tile(r, "rn"), x)[:, k0:k1],
+                in_=banks[("np", r, x)][:].rearrange("p (s k) -> p k s", s=SB)[:, k0:k1],
                 func=FN.Abs_reciprocal_sqrt,
             )
 
@@ -280,7 +282,8 @@ def tile_mpl_t_kernel(tc, p, q, W, out):
             bt, sh = divmod(r, HALVES)
             if r == ROUNDS - 1:
                 return
-            fin_part(nc.gpsimd, r, h * KH, (h + 1) * KH)
+            fin_part(nc.vector, r, h * KH, h * KH + VECTOR_K)
+            fin_part(nc.gpsimd, r, h * KH + VECTOR_K, (h + 1) * KH)
             if sh == HALVES - 1:
                 cols = slice(h * KH * S, (h + 1) * KH * S)
                 nc.sync.dma_start(out=out_flat[bt * P:(bt + 1) * P, cols], in_=tiles[("o", bt)][:, cols])
@@ -289,15 +292,14 @@ def tile_mpl_t_kernel(tc, p, q, W, out):
             c0 = k * S + r % HALVES * SH
             nc.vector.tensor_copy(out=warm[:], in_=tiles[("o", r // HALVES)][:, c0:c0 + 1])
 
-        def fin_last(r, kt):
-            if kt % 2 == 0:
-                after_gpsimd(r - 1, kt * P)
-            fin_part(nc.vector, r, kt * P, (kt + 1) * P)
-            if r == ROUNDS - 1:
-                cols = slice(kt * P * S, (kt + 1) * P * S)
-                nc.sync.dma_start(
-                    out=out_flat[(NBT - 1) * P:NBT * P, cols], in_=tiles[("o", NBT - 1)][:, cols]
-                )
+        def fin_last(r, k0, k1):
+            if k0 % KH == 0:
+                after_gpsimd(r - 1, k0 + VECTOR_K)
+            fin_part(nc.vector, r, k0, k1)
+            cols = slice(k0 * S, k1 * S)
+            nc.sync.dma_start(
+                out=out_flat[(NBT - 1) * P:NBT * P, cols], in_=tiles[("o", NBT - 1)][:, cols]
+            )
 
         for kt in range(NKT):
             t_w(kt // 2, kt % 2)
@@ -374,18 +376,21 @@ def tile_mpl_t_kernel(tc, p, q, W, out):
                 pq(r + 1, 2)
                 pq(r + 1, 3)
             else:
-                fin_last(r, 0)
+                fin_last(r, 0, P)
             mx(r, 2)
             mx(r, 3)
             dc(r, 2)
             if not nxt:
-                fin_last(r, 1)
+                fin_last(r, P, KH)
             dc(r, 3)
             rs(r, 2)
-            rs(r, 3)
-            if not nxt:
-                fin_last(r, 2)
-                fin_last(r, 3)
+            if nxt:
+                rs(r, 3)
+            else:
+                rs(r, 3, 0, P)
+                rs(r, 3, P, KH)
+                for k0 in range(KH, K, LAST_K):
+                    fin_last(r, k0, k0 + LAST_K)
             if late_q:
                 q_norms(bt + 1)
                 q_factor(bt + 1)

@@ -169,7 +169,9 @@ def tile_mpl_t_kernel(tc, p, q, W, out):
             copy_words(("q", bt), unit(q_raw, bt), bt > 0)
 
         def q_square(bt):
-            nc.vector.tensor_tensor(out=unit(q_sq, bt), in0=unit(q_raw, bt), in1=unit(q_raw, bt), op=ALU.mult)
+            nc.vector.tensor_tensor(
+                out=grouped(unit(q_sq, bt)), in0=bank_values(("q", bt)), in1=grouped(unit(q_raw, bt)), op=ALU.mult
+            )
 
         def q_quantise(bt):
             quantise(q_sq, q_codes, q_scales, bt, 1)
@@ -282,8 +284,13 @@ def tile_mpl_t_kernel(tc, p, q, W, out):
             bt, sh = divmod(r, HALVES)
             if r == ROUNDS - 1:
                 return
-            fin_part(nc.vector, r, h * KH, h * KH + VECTOR_K)
             fin_part(nc.gpsimd, r, h * KH + VECTOR_K, (h + 1) * KH)
+
+        def fin_rest(r, h):
+            bt, sh = divmod(r, HALVES)
+            if r == ROUNDS - 1:
+                return
+            fin_part(nc.vector, r, h * KH, h * KH + VECTOR_K)
             if sh == HALVES - 1:
                 cols = slice(h * KH * S, (h + 1) * KH * S)
                 nc.sync.dma_start(out=out_flat[bt * P:(bt + 1) * P, cols], in_=tiles[("o", bt)][:, cols])
@@ -349,8 +356,6 @@ def tile_mpl_t_kernel(tc, p, q, W, out):
             if nxt:
                 sq(r + 1, 2)
             quant(r, 1)
-            if late_q:
-                q_square(bt + 1)
             if r > 0:
                 fin(r - 1, 1)
             if nxt:
@@ -360,6 +365,8 @@ def tile_mpl_t_kernel(tc, p, q, W, out):
             mx(r, 1)
             dc(r, 0)
             dc(r, 1)
+            if r > 0:
+                fin_rest(r - 1, 1)
             rs(r, 0)
             if nxt:
                 sq(r + 1, 3)
@@ -380,9 +387,12 @@ def tile_mpl_t_kernel(tc, p, q, W, out):
             mx(r, 2)
             mx(r, 3)
             dc(r, 2)
+            if early_q:
+                q_square(bt + 1)
             if not nxt:
                 fin_last(r, P, KH)
             dc(r, 3)
+            fin_rest(r, 0)
             rs(r, 2)
             if nxt:
                 rs(r, 3)

@@ -26,6 +26,7 @@ BYTES = 2 * (B * S * D + B * D + K * D) + 4 * B * S * K
 
 LAST_K = 64
 PINNED = True
+LAST_VECTOR_K = 128
 VECTOR_K = 32
 KH = K // 2
 NKH = K // KH
@@ -39,8 +40,9 @@ def tile_mpl_t_kernel(tc, p, q, W, out):
         if PINNED:
             ctx.enter_context(tc.manual_schedule())
         const = ctx.enter_context(tc.tile_pool(name="const", bufs=1))
-        loads = ctx.enter_context(tc.tile_pool(name="loads", bufs=6))
+        loads = ctx.enter_context(tc.tile_pool(name="loads", bufs=5))
         prods = ctx.enter_context(tc.tile_pool(name="prods", bufs=2))
+        packed = ctx.enter_context(tc.tile_pool(name="packed", bufs=3))
         epi = ctx.enter_context(tc.tile_pool(name="epi", bufs=2))
         outs = ctx.enter_context(tc.tile_pool(name="outs", bufs=2))
         psx = ctx.enter_context(tc.psum_pool(name="psx", bufs=4))
@@ -165,8 +167,11 @@ def tile_mpl_t_kernel(tc, p, q, W, out):
                     stop=(g == PASSES - 1),
                 )
 
+        def t_q(bt):
+            transposes(("q", bt), unit(q_ld, bt))
+
         def q_copy(bt):
-            copy_words(("q", bt), unit(q_raw, bt), bt > 0)
+            copy_words(("q", bt), unit(q_raw, bt), bt > 1 or False)
 
         def q_square(bt):
             nc.vector.tensor_tensor(
@@ -186,13 +191,13 @@ def tile_mpl_t_kernel(tc, p, q, W, out):
             f = factor[:, bt * K:(bt + 1) * K]
             nc.scalar.activation(out=f, in_=banks[("nq", bt)][:], func=FN.Abs_reciprocal_sqrt)
 
-        def round_tile(r, name, shape, dtype):
+        def round_tile(pool, r, name, shape, dtype):
             if (name, r) not in tiles:
-                tiles[(name, r)] = prods.tile(shape, dtype, name=name, align_bytes=64)
+                tiles[(name, r)] = pool.tile(shape, dtype, name=name, align_bytes=64)
             return tiles[(name, r)]
 
         def prod_of(r):
-            return round_tile(r, "prod", [P, 2 * SH * D], BF16)
+            return round_tile(prods, r, "prod", [P, 2 * SH * D], BF16)
 
         def pp_unit(sl):
             return (sl // 2) * 4 + sl % 2
@@ -214,8 +219,8 @@ def tile_mpl_t_kernel(tc, p, q, W, out):
         def quant(r, half):
             quantise(
                 prod_of(r),
-                round_tile(r, "codes", [P, 2 * SH * WORDS], U32),
-                round_tile(r, "scales", [P, 2 * SH * WORDS], U8),
+                round_tile(packed, r, "codes", [P, 2 * SH * WORDS], U32),
+                round_tile(packed, r, "scales", [P, 2 * SH * WORDS], U8),
                 4 * half,
                 4,
             )
@@ -280,17 +285,15 @@ def tile_mpl_t_kernel(tc, p, q, W, out):
                 op=ALU.mult,
             )
 
+        def vector_k(r, h):
+            return LAST_VECTOR_K if (r, h) == (ROUNDS - 2, 1) else VECTOR_K
+
         def fin(r, h):
-            bt, sh = divmod(r, HALVES)
-            if r == ROUNDS - 1:
-                return
-            fin_part(nc.gpsimd, r, h * KH + VECTOR_K, (h + 1) * KH)
+            fin_part(nc.gpsimd, r, h * KH + vector_k(r, h), (h + 1) * KH)
 
         def fin_rest(r, h):
             bt, sh = divmod(r, HALVES)
-            if r == ROUNDS - 1:
-                return
-            fin_part(nc.vector, r, h * KH, h * KH + VECTOR_K)
+            fin_part(nc.vector, r, h * KH, h * KH + vector_k(r, h))
             if sh == HALVES - 1:
                 cols = slice(h * KH * S, (h + 1) * KH * S)
                 nc.sync.dma_start(out=out_flat[bt * P:(bt + 1) * P, cols], in_=tiles[("o", bt)][:, cols])
@@ -301,7 +304,7 @@ def tile_mpl_t_kernel(tc, p, q, W, out):
 
         def fin_last(r, k0, k1):
             if k0 % KH == 0:
-                after_gpsimd(r - 1, k0 + VECTOR_K)
+                after_gpsimd(r - 1, k0 + vector_k(r - 1, k0 // KH))
             fin_part(nc.vector, r, k0, k1)
             cols = slice(k0 * S, k1 * S)
             nc.sync.dma_start(
@@ -318,7 +321,7 @@ def tile_mpl_t_kernel(tc, p, q, W, out):
                 )
             else:
                 square_bank(("w", kt), unit(w_sq, kt))
-        transposes(("q", 0), unit(q_ld, 0))
+        t_q(0)
         t_p(0, 0)
         t_p(0, 1)
         t_p(0, 2)
@@ -342,71 +345,103 @@ def tile_mpl_t_kernel(tc, p, q, W, out):
         pq(0, 3)
         t_p(1, 2)
         t_p(1, 3)
+        sq(1, 0)
+        sq(1, 1)
+        quant(0, 1)
+        q_factor(0)
+        pq(1, 0)
+        pq(1, 1)
 
         def period(r):
-            nxt = r + 1 < ROUNDS
-            bt = r // HALVES
-            early_q = r % HALVES == 0 and bt + 1 < NBT
-            late_q = r % HALVES == 1 and bt + 1 < NBT
-            if nxt:
-                sq(r + 1, 0)
-                sq(r + 1, 1)
-            if r == 0:
-                q_factor(0)
-            if nxt:
-                sq(r + 1, 2)
-            quant(r, 1)
+            has1 = r + 1 < ROUNDS
+            has2 = r + 2 < ROUNDS
+            nq = (r + 3) // 2 if r % 2 == 1 else 0
+            nq = nq if nq < NBT else 0
+            mq = r // 2 + 1 if r % 2 == 0 and r // 2 + 1 < NBT else 0
+            mx(r, 0)
+            if has1:
+                quant(r + 1, 0)
             if r > 0:
                 fin(r - 1, 1)
-            if nxt:
-                pq(r + 1, 0)
-                pq(r + 1, 1)
-            mx(r, 0)
-            mx(r, 1)
+            if has1:
+                sq(r + 1, 2)
+                pq(r + 1, 2)
             dc(r, 0)
+            mx(r, 1)
+            if has1:
+                sq(r + 1, 3)
+                pq(r + 1, 3)
+            rs(r, 0)
+            rs(r, 1)
+            if r == 0:
+                t_q(1)
+                q_copy(1)
             dc(r, 1)
             if r > 0:
                 fin_rest(r - 1, 1)
-            rs(r, 0)
-            if nxt:
-                sq(r + 1, 3)
-            rs(r, 1)
-            if early_q:
-                transposes(("q", bt + 1), unit(q_ld, bt + 1))
-                q_copy(bt + 1)
-            if nxt:
-                quant(r + 1, 0)
-            if late_q:
-                q_quantise(bt + 1)
+            if has2:
+                t_p(r + 2, 0)
+                t_p(r + 2, 1)
+            if nq:
+                t_q(nq)
+            if has1:
+                quant(r + 1, 1)
+            if r == 1:
+                q_quantise(1)
+            if mq > 1:
+                q_quantise(mq)
             fin(r, 0)
-            if nxt:
-                pq(r + 1, 2)
-                pq(r + 1, 3)
-            else:
-                fin_last(r, 0, P)
+            if r == 0:
+                q_square(1)
             mx(r, 2)
-            mx(r, 3)
+            if has2:
+                sq(r + 2, 0)
+                pq(r + 2, 0)
             dc(r, 2)
-            if early_q:
-                q_square(bt + 1)
-            if not nxt:
-                fin_last(r, P, KH)
-            dc(r, 3)
-            fin_rest(r, 0)
+            mx(r, 3)
+            if has2:
+                sq(r + 2, 1)
+                pq(r + 2, 1)
             rs(r, 2)
-            if nxt:
-                rs(r, 3)
-            else:
-                rs(r, 3, 0, P)
-                rs(r, 3, P, KH)
-                for k0 in range(KH, K, LAST_K):
-                    fin_last(r, k0, k0 + LAST_K)
-            if late_q:
-                q_norms(bt + 1)
-                q_factor(bt + 1)
-            if r + 2 < ROUNDS:
-                for sl in range(SH):
-                    t_p(r + 2, sl)
+            if nq:
+                q_copy(nq)
+                q_square(nq)
+            dc(r, 3)
+            if has2:
+                fin_rest(r, 0)
+            rs(r, 3)
+            if mq > 1:
+                q_norms(mq)
+                q_factor(mq)
+            if r == 1:
+                q_norms(1)
+                q_factor(1)
+            if has2:
+                t_p(r + 2, 2)
+                t_p(r + 2, 3)
 
-        for r in range(ROUNDS):
+        def last_period(r):
+            fin(r - 1, 1)
+            mx(r, 0)
+            dc(r, 0)
+            mx(r, 1)
+            rs(r, 0)
+            rs(r, 1)
+            dc(r, 1)
+            fin_rest(r - 1, 0)
+            fin_last(r, 0, P)
+            fin_last(r, P, KH)
+            mx(r, 2)
+            dc(r, 2)
+            rs(r, 2)
+            mx(r, 3)
+            dc(r, 3)
+            rs(r, 3, 0, P)
+            rs(r, 3, P, KH)
+            fin_rest(r - 1, 1)
+            for k0 in range(KH, K, LAST_K):
+                fin_last(r, k0, k0 + LAST_K)
+
+        for r in range(ROUNDS - 1):
             period(r)
+        last_period(ROUNDS - 1)

@@ -77,9 +77,14 @@ def tile_mpl_t_kernel(tc, p, q, W, out):
                 )
             p_ld.append(ld)
 
-        for kt in range(NKT):
+        def load_w(kt):
             nc.sync.dma_start(out=w_ld[:, kt * D:(kt + 1) * D], in_=W[kt * P:(kt + 1) * P, :])
+
+        load_w(0)
+        load_w(1)
         load_q(0)
+        load_w(2)
+        load_w(3)
         load_p(0, SH)
         load_p(1, 1)
         for bt in range(1, NBT):
@@ -90,7 +95,7 @@ def tile_mpl_t_kernel(tc, p, q, W, out):
         w_sq = const.tile([P, NKT * D], BF16, name="w_sq", align_bytes=64)
         w_codes = const.tile([P, NKT * WORDS], U32, name="w_codes", align_bytes=64)
         w_scales = const.tile([P, NKT * WORDS], U8, name="w_scales", align_bytes=64)
-        w_raw = const.tile([P, 2 * D], BF16, name="w_raw")
+        w_nat = const.tile([P, 2 * D], BF16, name="w_nat")
         q_raw = const.tile([P, NBT * D], BF16, name="q_raw")
         q_sq = const.tile([P, NBT * D], BF16, name="q_sq", align_bytes=64)
         q_codes = const.tile([P, NBT * WORDS], U32, name="q_codes", align_bytes=64)
@@ -115,14 +120,26 @@ def tile_mpl_t_kernel(tc, p, q, W, out):
                     )
             banks[key] = xt
 
+        def halves_apart(ap):
+            return ap.rearrange("p (g c u e) -> p g u c e", g=PASSES, u=2, e=2)
+
+        def apart(ap):
+            return ap.rearrange("p (g u c e) -> p g u c e", g=PASSES, u=2, e=2)
+
+        def w_square(i):
+            for g in range(PASSES):
+                src = halves_apart(unit(w_ld, 2 + i))[:, g]
+                nc.vector.tensor_tensor(out=apart(unit(w_nat, i))[:, g], in0=src, in1=src, op=ALU.mult)
+
         def t_w(kh, g):
             xt = psx.tile([P, 512], F32, name="xt")
             for i in range(2):
-                words = unit(w_ld, 2 * kh + i).bitcast(F32)
+                words = (unit(w_ld, i) if kh == 0 else unit(w_nat, i)).bitcast(F32)
                 for u in range(2):
+                    w0 = g * 256 + u * P
                     nc.tensor.transpose(
                         out=xt[:, u * 256 + i * P:u * 256 + (i + 1) * P],
-                        in_=words[:, g * 256 + u:(g + 1) * 256:2],
+                        in_=words[:, g * 256 + u:(g + 1) * 256:2] if kh == 0 else words[:, w0:w0 + P],
                         identity=ident[:],
                     )
             banks[("w", 2 * kh + g)] = xt
@@ -311,21 +328,21 @@ def tile_mpl_t_kernel(tc, p, q, W, out):
                 out=out_flat[(NBT - 1) * P:NBT * P, cols], in_=tiles[("o", NBT - 1)][:, cols]
             )
 
-        for kt in range(NKT):
-            t_w(kt // 2, kt % 2)
-        for kt in range(NKT):
-            if kt == 2:
-                copy_words(("w", kt), unit(w_raw, kt // 2), False)
-                nc.vector.tensor_tensor(
-                    out=unit(w_sq, kt), in0=unit(w_raw, kt // 2), in1=unit(w_raw, kt // 2), op=ALU.mult
-                )
-            else:
-                square_bank(("w", kt), unit(w_sq, kt))
+        w_square(0)
+        w_square(1)
+        t_w(0, 0)
+        t_w(0, 1)
         t_q(0)
+        t_w(1, 0)
+        t_w(1, 1)
+        for x in range(2):
+            square_bank(("w", x), unit(w_sq, x))
+        q_copy(0)
+        copy_words(("w", 2), unit(w_sq, 2), True)
+        copy_words(("w", 3), unit(w_sq, 3), False)
         t_p(0, 0)
         t_p(0, 1)
         t_p(0, 2)
-        q_copy(0)
         q_square(0)
         quantise(w_sq, w_codes, w_scales, 0, 2)
         quantise(w_sq, w_codes, w_scales, 2, 2)
@@ -386,10 +403,8 @@ def tile_mpl_t_kernel(tc, p, q, W, out):
                 t_q(nq)
             if has1:
                 quant(r + 1, 1)
-            if r == 1:
-                q_quantise(1)
-            if mq > 1:
-                q_quantise(mq)
+            if r % 2 == 1 and (r + 1) // 2 < NBT:
+                q_quantise((r + 1) // 2)
             fin(r, 0)
             if r == 0:
                 q_square(1)
@@ -410,12 +425,9 @@ def tile_mpl_t_kernel(tc, p, q, W, out):
             if has2:
                 fin_rest(r, 0)
             rs(r, 3)
-            if mq > 1:
-                q_norms(mq)
-                q_factor(mq)
-            if r == 1:
-                q_norms(1)
-                q_factor(1)
+            if r % 2 == 1 and (r + 1) // 2 < NBT:
+                q_norms((r + 1) // 2)
+                q_factor((r + 1) // 2)
             if has2:
                 t_p(r + 2, 2)
                 t_p(r + 2, 3)

from contextlib import ExitStack

import concourse.mybir as mybir
from concourse.masks import make_identity

F32 = mybir.dt.float32
BF16 = mybir.dt.bfloat16
U32 = mybir.dt.uint32
U8 = mybir.dt.uint8
FP8X4 = mybir.dt.float8_e4m3fn_x4
FN = mybir.ActivationFunctionType
ALU = mybir.AluOpType

P = 128
B, S, D, K = 512, 8, 1024, 512
NBT = B // P
NKT = K // P
SH = 4
HALVES = S // SH
ROUNDS = NBT * HALVES
PASSES = D // 512
WORDS = D // 4

FLOPS = 2 * (2 * B * S + B) * K * D
BYTES = 2 * (B * S * D + B * D + K * D) + 4 * B * S * K

LAST_K = 64
PINNED = True
LAST_VECTOR_K = 128
VECTOR_K = 32
KH = K // 2
NKH = K // KH
SB = SH // 2


def tile_mpl_t_kernel(tc, p, q, W, out):
    nc = tc.nc
    out_flat = out.rearrange("b s k -> b (s k)")
    with ExitStack() as ctx:
        if PINNED:
            ctx.enter_context(tc.manual_schedule())
        const = ctx.enter_context(tc.tile_pool(name="const", bufs=1))
        loads = ctx.enter_context(tc.tile_pool(name="loads", bufs=5))
        prods = ctx.enter_context(tc.tile_pool(name="prods", bufs=2))
        packed = ctx.enter_context(tc.tile_pool(name="packed", bufs=3))
        epi = ctx.enter_context(tc.tile_pool(name="epi", bufs=2))
        outs = ctx.enter_context(tc.tile_pool(name="outs", bufs=2))
        psx = ctx.enter_context(tc.psum_pool(name="psx", bufs=4))
        psn = ctx.enter_context(tc.psum_pool(name="psn", bufs=2))
        psd = ctx.enter_context(tc.psum_pool(name="psd", bufs=2))

        one = const.tile([P, 1], F32, name="one")
        warm = const.tile([P, 1], F32, name="warm")
        nc.vector.memset(one[:], 1.0)
        nc.scalar.activation(out=warm[:], in_=one[:], func=FN.Abs_reciprocal_sqrt)

        ident = const.tile([P, P], F32, name="ident")
        make_identity(nc, ident[:])

        w_ld = const.tile([P, NKT * D], BF16, name="w_ld")
        q_ld = const.tile([P, NBT * D], BF16, name="q_ld")
        p_ld = []

        def load_q(bt):
            nc.sync.dma_start(out=q_ld[:, bt * D:(bt + 1) * D], in_=q[bt * P:(bt + 1) * P, S - 1, :])

        def load_p(r, pieces):
            bt, sh = divmod(r, HALVES)
            ld = loads.tile([P, SH * D], BF16, name="ld")
            n = SH // pieces
            for i in range(pieces):
                nc.sync.dma_start(
                    out=ld[:, i * n * D:(i + 1) * n * D],
                    in_=p[bt * P:(bt + 1) * P, sh * SH + i * n:sh * SH + (i + 1) * n, :].rearrange(
                        "b s d -> b (s d)"
                    ),
                )
            p_ld.append(ld)

        def load_w(kt):
            nc.sync.dma_start(out=w_ld[:, kt * D:(kt + 1) * D], in_=W[kt * P:(kt + 1) * P, :])

        load_w(0)
        load_w(1)
        load_q(0)
        load_w(2)
        load_w(3)
        load_p(0, SH)
        load_p(1, 1)
        for bt in range(1, NBT):
            load_q(bt)
        for r in range(2, ROUNDS):
            load_p(r, 1)

        w_sq = const.tile([P, NKT * D], BF16, name="w_sq", align_bytes=64)
        w_codes = const.tile([P, NKT * WORDS], U32, name="w_codes", align_bytes=64)
        w_scales = const.tile([P, NKT * WORDS], U8, name="w_scales", align_bytes=64)
        w_nat = const.tile([P, 2 * D], BF16, name="w_nat")
        q_raw = const.tile([P, NBT * D], BF16, name="q_raw")
        q_sq = const.tile([P, NBT * D], BF16, name="q_sq", align_bytes=64)
        q_codes = const.tile([P, NBT * WORDS], U32, name="q_codes", align_bytes=64)
        q_scales = const.tile([P, NBT * WORDS], U8, name="q_scales", align_bytes=64)
        factor = const.tile([P, NBT * K], F32, name="factor")

        banks = {}
        tiles = {}

        def unit(ap, i):
            return ap[:, i * D:(i + 1) * D]

        def transposes(key, src):
            xt = psx.tile([P, 512], F32, name="xt")
            words = src.bitcast(F32)
            for g in range(PASSES):
                for u in range(2):
                    nc.tensor.transpose(
                        out=xt[:, u * 256 + g * P:u * 256 + (g + 1) * P],
                        in_=words[:, g * 256 + u:(g + 1) * 256:2],
                        identity=ident[:],
                    )
            banks[key] = xt

        def halves_apart(ap):
            return ap.rearrange("p (g c u e) -> p g u c e", g=PASSES, u=2, e=2)

        def apart(ap):
            return ap.rearrange("p (g u c e) -> p g u c e", g=PASSES, u=2, e=2)

        def w_square(i):
            for g in range(PASSES):
                src = halves_apart(unit(w_ld, 2 + i))[:, g]
                nc.vector.tensor_tensor(out=apart(unit(w_nat, i))[:, g], in0=src, in1=src, op=ALU.mult)

        def t_w(kh, g):
            xt = psx.tile([P, 512], F32, name="xt")
            for i in range(2):
                words = (unit(w_ld, i) if kh == 0 else unit(w_nat, i)).bitcast(F32)
                for u in range(2):
                    w0 = g * 256 + u * P
                    nc.tensor.transpose(
                        out=xt[:, u * 256 + i * P:u * 256 + (i + 1) * P],
                        in_=words[:, g * 256 + u:(g + 1) * 256:2] if kh == 0 else words[:, w0:w0 + P],
                        identity=ident[:],
                    )
            banks[("w", 2 * kh + g)] = xt

        def t_p(r, sl):
            transposes(("p", r, sl), unit(p_ld[r], sl))

        def bank_values(key):
            return banks[key][:].bitcast(BF16).rearrange("p (u c e) -> p c u e", u=2, e=2)

        def grouped(ap):
            return ap.rearrange("p (c u e) -> p c u e", u=2, e=2)

        def copy_words(key, dst, on_scalar):
            copy = nc.scalar.copy if on_scalar else nc.vector.tensor_copy
            copy(
                out=dst.bitcast(F32).rearrange("p (c u) -> p c u", u=2),
                in_=banks[key][:].rearrange("p (u c) -> p c u", u=2),
            )

        def square_bank(key, dst):
            nc.scalar.activation(out=grouped(dst), in_=bank_values(key), func=FN.Square)

        def quantise(src, codes, scales, first, count):
            nc.vector.quantize_mx(
                out=codes[:, first * WORDS:(first + count) * WORDS].bitcast(FP8X4),
                scales=scales[:, first * WORDS:(first + count) * WORDS],
                in_=src[:, first * D:(first + count) * D],
            )

        def mx_group(dst, a_codes, a_scales, a_unit, kh):
            for g in range(PASSES):
                a0 = a_unit * WORDS + g * P
                w0 = (kh * PASSES + g) * KH
                nc.tensor.matmul_mx(
                    out=dst,
                    lhsT=a_codes[:, a0:a0 + P].bitcast(FP8X4),
                    lhsT_scale=a_scales[:, a0:a0 + P],
                    rhs=w_codes[:, w0:w0 + KH].bitcast(FP8X4),
                    rhs_scale=w_scales[:, w0:w0 + KH],
                    start=(g == 0),
                    stop=(g == PASSES - 1),
                )

        def t_q(bt):
            transposes(("q", bt), unit(q_ld, bt))

        def q_copy(bt):
            copy_words(("q", bt), unit(q_raw, bt), bt > 1 or False)

        def q_square(bt):
            nc.vector.tensor_tensor(
                out=grouped(unit(q_sq, bt)), in0=bank_values(("q", bt)), in1=grouped(unit(q_raw, bt)), op=ALU.mult
            )

        def q_quantise(bt):
            quantise(q_sq, q_codes, q_scales, bt, 1)

        def q_norms(bt):
            nq = psn.tile([P, K], F32, name="npb")
            for kh in range(NKH):
                mx_group(nq[:, kh * KH:(kh + 1) * KH], q_codes, q_scales, bt, kh)
            banks[("nq", bt)] = nq

        def q_factor(bt):
            f = factor[:, bt * K:(bt + 1) * K]
            nc.scalar.activation(out=f, in_=banks[("nq", bt)][:], func=FN.Abs_reciprocal_sqrt)

        def round_tile(pool, r, name, shape, dtype):
            if (name, r) not in tiles:
                tiles[(name, r)] = pool.tile(shape, dtype, name=name, align_bytes=64)
            return tiles[(name, r)]

        def prod_of(r):
            return round_tile(prods, r, "prod", [P, 2 * SH * D], BF16)

        def pp_unit(sl):
            return (sl // 2) * 4 + sl % 2

        def pq_unit(sl):
            return (sl // 2) * 4 + 2 + sl % 2

        def sq(r, sl):
            square_bank(("p", r, sl), unit(prod_of(r), pp_unit(sl)))

        def pq(r, sl):
            nc.vector.tensor_tensor(
                out=grouped(unit(prod_of(r), pq_unit(sl))),
                in0=bank_values(("p", r, sl)),
                in1=grouped(unit(q_raw, r // HALVES)),
                op=ALU.mult,
            )

        def quant(r, half):
            quantise(
                prod_of(r),
                round_tile(packed, r, "codes", [P, 2 * SH * WORDS], U32),
                round_tile(packed, r, "scales", [P, 2 * SH * WORDS], U8),
                4 * half,
                4,
            )

        def mx(r, x):
            codes = tiles[("codes", r)]
            scales = tiles[("scales", r)]
            kh, pair = divmod(x, 2)
            dtb = psd.tile([P, SB * KH], F32, name="dtb")
            for i in range(SB):
                mx_group(dtb[:, i * KH:(i + 1) * KH], codes, scales, pq_unit(pair * SB + i), kh)
            npb = psn.tile([P, SB * KH], F32, name="npb")
            for i in range(SB):
                mx_group(npb[:, i * KH:(i + 1) * KH], codes, scales, pp_unit(pair * SB + i), kh)
            banks[("dot", r, x)] = dtb
            banks[("np", r, x)] = npb

        def epi_tile(r, name):
            if (name, r) not in tiles:
                tiles[(name, r)] = epi.tile([P, K * SH], F32, name=name)
            return tiles[(name, r)]

        def ks(ap, s):
            return ap.rearrange("p (k s) -> p k s", s=s)

        def part(ap, x):
            return ks(ap[:, x * KH * SB:(x + 1) * KH * SB], SB)

        def rs(r, x, k0=0, k1=KH):
            nc.scalar.activation(
                out=part(epi_tile(r, "rn"), x)[:, k0:k1],
                in_=banks[("np", r, x)][:].rearrange("p (s k) -> p k s", s=SB)[:, k0:k1],
                func=FN.Abs_reciprocal_sqrt,
            )

        def dc(r, x):
            f0 = r // HALVES * K + x // 2 * KH
            nc.vector.scalar_tensor_tensor(
                out=part(epi_tile(r, "dc"), x),
                in0=banks[("dot", r, x)][:].rearrange("p (s k) -> p k s", s=SB),
                scalar=-1.0 / D,
                in1=factor[:, f0:f0 + KH].unsqueeze(2).to_broadcast([P, KH, SB]),
                op0=ALU.mult,
                op1=ALU.mult,
            )

        def fin_part(eng, r, k0, k1):
            bt, sh = divmod(r, HALVES)
            if ("o", bt) not in tiles:
                tiles[("o", bt)] = outs.tile([P, K * S], F32, name="o_sb")
            kh = k0 // KH

            def both_pairs(name):
                half = tiles[(name, r)][:, kh * KH * SH:(kh + 1) * KH * SH]
                return half.rearrange("p (a k s) -> p k a s", a=2, s=SB)[:, k0 - kh * KH:k1 - kh * KH]

            o = ks(tiles[("o", bt)][:, k0 * S:k1 * S], S)[:, :, sh * SH:(sh + 1) * SH]
            eng.tensor_tensor(
                out=o.rearrange("p k (a s) -> p k a s", a=2),
                in0=both_pairs("dc"),
                in1=both_pairs("rn"),
                op=ALU.mult,
            )

        def vector_k(r, h):
            return LAST_VECTOR_K if (r, h) == (ROUNDS - 2, 1) else VECTOR_K

        def fin(r, h):
            fin_part(nc.gpsimd, r, h * KH + vector_k(r, h), (h + 1) * KH)

        def fin_rest(r, h):
            bt, sh = divmod(r, HALVES)
            fin_part(nc.vector, r, h * KH, h * KH + vector_k(r, h))
            if sh == HALVES - 1:
                cols = slice(h * KH * S, (h + 1) * KH * S)
                nc.sync.dma_start(out=out_flat[bt * P:(bt + 1) * P, cols], in_=tiles[("o", bt)][:, cols])

        def after_gpsimd(r, k):
            c0 = k * S + r % HALVES * SH
            nc.vector.tensor_copy(out=warm[:], in_=tiles[("o", r // HALVES)][:, c0:c0 + 1])

        def fin_last(r, k0, k1):
            if k0 % KH == 0:
                after_gpsimd(r - 1, k0 + vector_k(r - 1, k0 // KH))
            fin_part(nc.vector, r, k0, k1)
            cols = slice(k0 * S, k1 * S)
            nc.sync.dma_start(
                out=out_flat[(NBT - 1) * P:NBT * P, cols], in_=tiles[("o", NBT - 1)][:, cols]
            )

        w_square(0)
        w_square(1)
        t_w(0, 0)
        t_w(0, 1)
        t_q(0)
        t_w(1, 0)
        t_w(1, 1)
        for x in range(2):
            square_bank(("w", x), unit(w_sq, x))
        q_copy(0)
        copy_words(("w", 2), unit(w_sq, 2), True)
        copy_words(("w", 3), unit(w_sq, 3), False)
        t_p(0, 0)
        t_p(0, 1)
        t_p(0, 2)
        q_square(0)
        quantise(w_sq, w_codes, w_scales, 0, 2)
        quantise(w_sq, w_codes, w_scales, 2, 2)
        q_quantise(0)
        t_p(0, 3)
        sq(0, 0)
        sq(0, 1)
        pq(0, 0)
        pq(0, 1)
        t_p(1, 0)
        t_p(1, 1)
        q_norms(0)
        sq(0, 2)
        quant(0, 0)
        sq(0, 3)
        pq(0, 2)
        pq(0, 3)
        t_p(1, 2)
        t_p(1, 3)
        sq(1, 0)
        sq(1, 1)
        quant(0, 1)
        q_factor(0)
        pq(1, 0)
        pq(1, 1)

        def period(r):
            has1 = r + 1 < ROUNDS
            has2 = r + 2 < ROUNDS
            nq = (r + 3) // 2 if r % 2 == 1 else 0
            nq = nq if nq < NBT else 0
            mq = r // 2 + 1 if r % 2 == 0 and r // 2 + 1 < NBT else 0
            mx(r, 0)
            if has1:
                quant(r + 1, 0)
            if r > 0:
                fin(r - 1, 1)
            if has1:
                sq(r + 1, 2)
                pq(r + 1, 2)
            dc(r, 0)
            mx(r, 1)
            if has1:
                sq(r + 1, 3)
                pq(r + 1, 3)
            rs(r, 0)
            rs(r, 1)
            if r == 0:
                t_q(1)
                q_copy(1)
            dc(r, 1)
            if r > 0:
                fin_rest(r - 1, 1)
            if has2:
                t_p(r + 2, 0)
                t_p(r + 2, 1)
            if nq:
                t_q(nq)
            if has1:
                quant(r + 1, 1)
            if r % 2 == 1 and (r + 1) // 2 < NBT:
                q_quantise((r + 1) // 2)
            fin(r, 0)
            if r == 0:
                q_square(1)
            mx(r, 2)
            if has2:
                sq(r + 2, 0)
                pq(r + 2, 0)
            dc(r, 2)
            mx(r, 3)
            if has2:
                sq(r + 2, 1)
                pq(r + 2, 1)
            rs(r, 2)
            if nq:
                q_copy(nq)
                q_square(nq)
            dc(r, 3)
            if has2:
                fin_rest(r, 0)
            rs(r, 3)
            if r % 2 == 1 and (r + 1) // 2 < NBT:
                q_norms((r + 1) // 2)
                q_factor((r + 1) // 2)
            if has2:
                t_p(r + 2, 2)
                t_p(r + 2, 3)

        def last_period(r):
            fin(r - 1, 1)
            mx(r, 0)
            dc(r, 0)
            mx(r, 1)
            rs(r, 0)
            rs(r, 1)
            dc(r, 1)
            fin_rest(r - 1, 0)
            fin_last(r, 0, P)
            fin_last(r, P, KH)
            mx(r, 2)
            dc(r, 2)
            rs(r, 2)
            mx(r, 3)
            dc(r, 3)
            rs(r, 3, 0, P)
            rs(r, 3, P, KH)
            fin_rest(r - 1, 1)
            for k0 in range(KH, K, LAST_K):
                fin_last(r, k0, k0 + LAST_K)

        for r in range(ROUNDS - 1):
            period(r)
        last_period(ROUNDS - 1)
